import numpy as np
import ml_dtypes

BF16 = ml_dtypes.bfloat16


def bf(x):
    return np.asarray(x, np.float32).astype(BF16)


def f32(x):
    return np.asarray(x, np.float32)


def f64(x):
    return np.asarray(x).astype(np.float64)


def striped(idx):
    return np.tile(idx.reshape(-1, 16).T, (8, 1))


S, D, M, F, ND, B, L, P, N = 4096, 128, 512, 2048, 1024, 8, 16, 128, 2048
EPS, SLOPE = 1e-5, 0.01


def lrelu(v):
    return np.maximum(v, SLOPE * v)


def setup_inputs():
    return {
        "table": bf(np.random.standard_normal((S, D))),
        "w": bf(np.random.standard_normal((D, M)) / np.sqrt(2.0 * D)),
        "x": bf(np.random.standard_normal((ND, P))),
        "w_dst": bf(np.random.standard_normal((ND, M)) / np.sqrt(4.0 * ND)),
        "w_src": bf(np.random.standard_normal((ND, M)) / np.sqrt(4.0 * ND)),
        "b1": f32(0.1 * np.random.standard_normal((M, 1))),
        "w2": bf(np.random.standard_normal((M, F)) / np.sqrt(M)),
        "b2": f32(0.1 * np.random.standard_normal((F, 1))),
        "wu": bf(np.random.standard_normal((F, ND)) / np.sqrt(L * F)),
        "bu": f32(0.1 * np.random.standard_normal((ND, 1))),
        "gamma": f32(1.0 + 0.1 * np.random.standard_normal((ND, 1))),
        "beta": f32(0.1 * np.random.standard_normal((ND, 1))),
        "offs": striped(np.random.permutation(S)[:N]),
    }


def reference(table, w, x, w_dst, w_src, b1, w2, b2, wu, bu, gamma, beta, offs):
    idx = offs[:16].T.reshape(-1)
    e = f64(w).T @ f64(table)[idx].T
    r = f64(w_dst).T @ f64(x)
    q = f64(w_src).T @ f64(x)
    pre = e.reshape(M, B, L, L) + r.reshape(M, B, L)[:, :, :, None] + q.reshape(M, B, L)[:, :, None, :] + f64(b1)[:, :, None, None]
    h = lrelu(pre).reshape(M, N)
    msg = lrelu(f64(w2).T @ h + f64(b2))
    agg = msg.reshape(F, P, L).sum(axis=2)
    u = lrelu(f64(wu).T @ agg + f64(bu))
    y = f64(x) + u
    mu = y.mean(axis=0, keepdims=True)
    var = ((y - mu) ** 2).mean(axis=0, keepdims=True)
    return (y - mu) / np.sqrt(var + EPS) * f64(gamma) + f64(beta)

@@ -1,0 +1,274 @@
+from contextlib import ExitStack
+
+import concourse.mybir as mybir
+from concourse.masks import make_identity
+
+BF16 = mybir.dt.bfloat16
+F32 = mybir.dt.float32
+U16 = mybir.dt.uint16
+ALU = mybir.AluOpType
+FUNC = mybir.ActivationFunctionType
+AXIS = mybir.AxisListType
+
+P = 128
+S = 4096
+M = 512
+F = 2048
+ND = 1024
+N = 2048
+L = 16
+PIECE = 512
+SLOPE = 0.01
+EPS = 1e-5
+
+M_BLOCKS = M // P
+F_BLOCKS = F // P
+D_BLOCKS = ND // P
+PIECES = N // PIECE
+NODES = PIECE // L
+
+FLOPS = 2 * (P * M * N + 2 * ND * M * P + M * F * N + F * ND * P)
+
+
+def tile_proteindecoder_b_kernel(
+    tc, table, w, x, w_dst, w_src, b1, w2, b2, wu, bu, gamma, beta, offs, out
+):
+    nc = tc.nc
+    with ExitStack() as ctx:
+        held = ctx.enter_context(tc.tile_pool(name="held", bufs=1))
+        work = ctx.enter_context(tc.tile_pool(name="work", bufs=3))
+        terms = ctx.enter_context(tc.tile_pool(name="terms", bufs=4))
+        psum = ctx.enter_context(tc.psum_pool(name="psum", bufs=8))
+
+        offsets = held.tile([P, N // 16], U16, name="offsets")
+        nc.sync.dma_start(offsets[:], offs)
+
+        table_blocks = table.rearrange("(b p) k -> p b k", p=P)
+        table_rows = []
+        for g in range(4):
+            rows = held.tile([P, 8, P], BF16, name=f"table_rows{g}")
+            nc.sync.dma_start(rows[:], table_blocks[:, 8 * g : 8 * (g + 1), :])
+            table_rows.append(rows)
+
+        x_sb = held.tile([P, D_BLOCKS, P], BF16, name="x_sb")
+        nc.scalar.dma_start(x_sb[:], x.rearrange("(c p) n -> p c n", p=P))
+        wdst_sb = held.tile([P, D_BLOCKS, M], BF16, name="wdst_sb")
+        nc.scalar.dma_start(wdst_sb[:], w_dst.rearrange("(c p) m -> p c m", p=P))
+        w_sb = held.tile([P, M], BF16, name="w_sb")
+        nc.scalar.dma_start(w_sb[:], w)
+
+        vec_rows = held.tile([P, P], F32, name="vec_rows")
+        nc.vector.memset(vec_rows[:], 0.0)
+        first_row = {}
+        row = 0
+        for key, vec in (("b1", b1), ("b2", b2), ("bu", bu), ("gamma", gamma), ("beta", beta)):
+            blocks = vec.shape[0] // P
+            nc.gpsimd.dma_start(
+                vec_rows[row : row + blocks, :], vec.rearrange("(r c) o -> r (c o)", c=P)
+            )
+            first_row[key] = row
+            row += blocks
+        wsrc_sb = held.tile([P, D_BLOCKS, M], BF16, name="wsrc_sb")
+        nc.gpsimd.dma_start(wsrc_sb[:], w_src.rearrange("(c p) m -> p c m", p=P))
+
+        w2_blocks = w2.rearrange("(c p) f -> p c f", p=P)
+        w2_sb = []
+        for g in range(4):
+            part = held.tile([P, M_BLOCKS, 4 * P], BF16, name=f"w2_sb{g}")
+            nc.sync.dma_start(part[:], w2_blocks[:, :, 4 * P * g : 4 * P * (g + 1)])
+            w2_sb.append(part)
+        wu_blocks = wu.rearrange("(b p) d -> p b d", p=P)
+        wu_sb = []
+        for g in range(4):
+            part = held.tile([P, 4, ND], BF16, name=f"wu_sb{g}")
+            nc.sync.dma_start(part[:], wu_blocks[:, 4 * g : 4 * (g + 1), :])
+            wu_sb.append(part)
+
+        ident_bf = held.tile([P, P], BF16, name="ident_bf")
+        make_identity(nc, ident_bf[:])
+        ident_f32 = held.tile([P, P], F32, name="ident_f32")
+        make_identity(nc, ident_f32[:])
+        mean_weights = held.tile([P, P], F32, name="mean_weights")
+        nc.vector.memset(mean_weights[:], 1.0 / ND)
+        eps_col = held.tile([P, 1], F32, name="eps_col")
+        nc.vector.memset(eps_col[:], EPS)
+
+        vec_ps = psum.tile([P, P], F32, name="vec_ps", tag="bank")
+        nc.tensor.transpose(vec_ps[:], vec_rows[:], ident_f32[:])
+        vec_cols = held.tile([P, P], F32, name="vec_cols")
+        nc.vector.tensor_copy(vec_cols[:], vec_ps[:])
+        slope_cols = held.tile([P, P], F32, name="slope_cols")
+        nc.vector.tensor_scalar(slope_cols[:], vec_cols[:], SLOPE, None, ALU.mult)
+
+        def col(key, block):
+            c = first_row[key] + block
+            return vec_cols[:, c : c + 1]
+
+        def slope_col(key, block):
+            c = first_row[key] + block
+            return slope_cols[:, c : c + 1]
+
+        table_t = held.tile([P, S], BF16, name="table_t")
+        for g in range(4):
+            flipped = psum.tile([P, 8 * P], BF16, name="flipped", tag="bank")
+            for b in range(8):
+                nc.tensor.transpose(
+                    flipped[:, b * P : (b + 1) * P], table_rows[g][:, b, :], ident_bf[:]
+                )
+            target = table_t[:, 8 * P * g : 8 * P * (g + 1)]
+            if g % 2 == 0:
+                nc.vector.tensor_copy(target, flipped[:])
+            else:
+                nc.scalar.copy(target, flipped[:])
+
+        r_ps = psum.tile([P, M], F32, name="r_ps", tag="bank")
+        q_ps = psum.tile([P, M], F32, name="q_ps", tag="bank")
+        for ps, weights in ((r_ps, wdst_sb), (q_ps, wsrc_sb)):
+            for mb in range(M_BLOCKS):
+                for c in range(D_BLOCKS):
+                    nc.tensor.matmul(
+                        ps[:, mb * P : (mb + 1) * P],
+                        weights[:, c, mb * P : (mb + 1) * P],
+                        x_sb[:, c, :],
+                        start=(c == 0),
+                        stop=(c == D_BLOCKS - 1),
+                    )
+        rb_sb = held.tile([P, M], F32, name="rb_sb")
+        for mb in range(M_BLOCKS):
+            nc.scalar.activation(
+                rb_sb[:, mb * P : (mb + 1) * P],
+                r_ps[:, mb * P : (mb + 1) * P],
+                FUNC.Identity,
+                bias=col("b1", mb),
+            )
+        q_sb = held.tile([P, M], F32, name="q_sb")
+        nc.vector.tensor_copy(q_sb[:], q_ps[:])
+
+        edge = []
+        for p in range(PIECES):
+            edge_p = held.tile([P, M_BLOCKS, PIECE], F32, name=f"edge{p}")
+            for mb in range(M_BLOCKS):
+                e_ps = psum.tile([P, PIECE], F32, name="e_ps", tag="bank")
+                nc.tensor.matmul(
+                    e_ps[:],
+                    w_sb[:, mb * P : (mb + 1) * P],
+                    table_t[:].indirect(offsets[:, (PIECE // 16) * p : (PIECE // 16) * (p + 1)]),
+                    start=True,
+                    stop=True,
+                )
+                if mb % 2 == 0:
+                    nc.scalar.copy(edge_p[:, mb, :], e_ps[:])
+                else:
+                    nc.vector.tensor_copy(edge_p[:, mb, :], e_ps[:])
+            edge.append(edge_p)
+
+        hidden = [None] * PIECES
+
+        def hidden_stage(p):
+            hidden[p] = held.tile([P, M_BLOCKS, PIECE], BF16, name=f"hidden{p}")
+            for mb in range(M_BLOCKS):
+                nodes = slice(mb * P + NODES * p, mb * P + NODES * (p + 1))
+                shape = [P, NODES // L, L, L]
+                node_terms = terms.tile([P, PIECE], F32, name="node_terms")
+                nc.gpsimd.tensor_tensor(
+                    node_terms[:].rearrange("q (g i t) -> q g i t", i=L, t=L),
+                    rb_sb[:, nodes].rearrange("q (g i) -> q g i", i=L).unsqueeze(3).to_broadcast(shape),
+                    q_sb[:, nodes].rearrange("q (g t) -> q g t", t=L).unsqueeze(2).to_broadcast(shape),
+                    ALU.add,
+                )
+                pre = work.tile([P, PIECE], F32, name="pre")
+                nc.vector.tensor_tensor(pre[:], edge[p][:, mb, :], node_terms[:], ALU.add)
+                nc.vector.scalar_tensor_tensor(
+                    hidden[p][:, mb, :], pre[:], SLOPE, pre[:], ALU.mult, ALU.max
+                )
+
+        agg = held.tile([P, F_BLOCKS, P], BF16, name="agg")
+
+        def message_stage(p):
+            for fb in range(F_BLOCKS):
+                m_ps = psum.tile([P, PIECE], F32, name="m_ps", tag="bank")
+                for c in range(M_BLOCKS):
+                    nc.tensor.matmul(
+                        m_ps[:],
+                        w2_sb[fb // 4][:, c, (fb % 4) * P : (fb % 4 + 1) * P],
+                        hidden[p][:, c, :],
+                        start=(c == 0),
+                        stop=(c == M_BLOCKS - 1),
+                    )
+                low = work.tile([P, PIECE], F32, name="low")
+                nc.scalar.activation(
+                    low[:], m_ps[:], FUNC.Identity, bias=slope_col("b2", fb), scale=SLOPE
+                )
+                msg = work.tile([P, PIECE], F32, name="msg")
+                nc.vector.scalar_tensor_tensor(
+                    msg[:], m_ps[:], col("b2", fb), low[:], ALU.add, ALU.max
+                )
+                with nc.allow_low_precision(reason="summed in float32, rounded once to bfloat16"):
+                    nc.vector.tensor_reduce(
+                        agg[:, fb, NODES * p : NODES * (p + 1)],
+                        msg[:].rearrange("q (n t) -> q n t", t=L),
+                        AXIS.X,
+                        ALU.add,
+                    )
+
+        hidden_stage(0)
+        for p in range(PIECES):
+            if p + 1 < PIECES:
+                hidden_stage(p + 1)
+            message_stage(p)
+
+        y = held.tile([P, D_BLOCKS, P], F32, name="y")
+        mean_ps = psum.tile([P, P], F32, name="mean_ps", tag="bank")
+
+        def add_to_mean(db):
+            nc.tensor.matmul(
+                mean_ps[:], mean_weights[:], y[:, db, :], start=(db == 0), stop=(db == D_BLOCKS - 1)
+            )
+
+        for db in range(D_BLOCKS):
+            u_ps = psum.tile([P, P], F32, name="u_ps", tag="bank")
+            for fb in range(F_BLOCKS):
+                nc.tensor.matmul(
+                    u_ps[:],
+                    wu_sb[fb // 4][:, fb % 4, db * P : (db + 1) * P],
+                    agg[:, fb, :],
+                    start=(fb == 0),
+                    stop=(fb == F_BLOCKS - 1),
+                )
+            u_low = work.tile([P, P], F32, name="u_low")
+            nc.scalar.activation(
+                u_low[:], u_ps[:], FUNC.Identity, bias=slope_col("bu", db), scale=SLOPE
+            )
+            u_sb = work.tile([P, P], F32, name="u_sb")
+            nc.vector.scalar_tensor_tensor(
+                u_sb[:], u_ps[:], col("bu", db), u_low[:], ALU.add, ALU.max
+            )
+            nc.vector.tensor_tensor(y[:, db, :], u_sb[:], x_sb[:, db, :], ALU.add)
+            if db > 0:
+                add_to_mean(db - 1)
+        add_to_mean(D_BLOCKS - 1)
+
+        centred = held.tile([P, D_BLOCKS, P], F32, name="centred")
+        squares = held.tile([P, D_BLOCKS, P], F32, name="squares")
+        var_ps = psum.tile([P, P], F32, name="var_ps", tag="bank")
+        for db in range(D_BLOCKS):
+            nc.vector.tensor_tensor(centred[:, db, :], y[:, db, :], mean_ps[:], ALU.subtract)
+            nc.scalar.activation(squares[:, db, :], centred[:, db, :], FUNC.Square)
+            nc.tensor.matmul(
+                var_ps[:], mean_weights[:], squares[:, db, :], start=(db == 0), stop=(db == D_BLOCKS - 1)
+            )
+        std = held.tile([P, P], F32, name="std")
+        nc.scalar.activation(std[:], var_ps[:], FUNC.Sqrt, bias=eps_col[:])
+        rstd = held.tile([P, P], F32, name="rstd")
+        nc.vector.reciprocal(rstd[:], std[:])
+
+        out_blocks = out.rearrange("(c p) n -> p c n", p=P)
+        result = held.tile([P, D_BLOCKS, P], F32, name="result")
+        for db in range(D_BLOCKS):
+            scaled = work.tile([P, P], F32, name="scaled")
+            nc.vector.scalar_tensor_tensor(
+                scaled[:], centred[:, db, :], col("gamma", db), rstd[:], ALU.mult, ALU.mult
+            )
+            nc.scalar.activation(result[:, db, :], scaled[:], FUNC.Identity, bias=col("beta", db))
+            if db % 4 == 3:
+                nc.sync.dma_start(out_blocks[:, db - 3 : db + 1, :], result[:, db - 3 : db + 1, :])

@@ -40,58 +40,72 @@ def tile_proteindecoder_b_kernel(
         terms = ctx.enter_context(tc.tile_pool(name="terms", bufs=4))
         psum = ctx.enter_context(tc.psum_pool(name="psum", bufs=8))
 
-        offsets = held.tile([P, N // 16], U16, name="offsets")
-        nc.sync.dma_start(offsets[:], offs)
+        ident_bf = held.tile([P, P], BF16, name="ident_bf")
+        make_identity(nc, ident_bf[:])
+        ident_f32 = held.tile([P, P], F32, name="ident_f32")
+        make_identity(nc, ident_f32[:])
 
         table_blocks = table.rearrange("(b p) k -> p b k", p=P)
-        table_rows = []
-        for g in range(4):
-            rows = held.tile([P, 8, P], BF16, name=f"table_rows{g}")
-            nc.sync.dma_start(rows[:], table_blocks[:, 8 * g : 8 * (g + 1), :])
-            table_rows.append(rows)
-
-        x_sb = held.tile([P, D_BLOCKS, P], BF16, name="x_sb")
-        nc.scalar.dma_start(x_sb[:], x.rearrange("(c p) n -> p c n", p=P))
-        wdst_sb = held.tile([P, D_BLOCKS, M], BF16, name="wdst_sb")
-        nc.scalar.dma_start(wdst_sb[:], w_dst.rearrange("(c p) m -> p c m", p=P))
+        w2_blocks = w2.rearrange("(c p) f -> p c f", p=P)
+        wu_blocks = wu.rearrange("(b p) d -> p b d", p=P)
+        table_rows = [held.tile([P, S // P // 2, P], BF16, name=f"table_rows{g}") for g in range(2)]
+        w2_sb = [held.tile([P, M_BLOCKS, F // 2], BF16, name=f"w2_sb{g}") for g in range(2)]
+        wu_sb = [held.tile([P, F_BLOCKS // 2, ND], BF16, name=f"wu_sb{g}") for g in range(2)]
+        offsets = held.tile([P, N // 16], U16, name="offsets")
         w_sb = held.tile([P, M], BF16, name="w_sb")
+        x_sb = held.tile([P, D_BLOCKS, P], BF16, name="x_sb")
+        wdst_sb = held.tile([P, D_BLOCKS, M], BF16, name="wdst_sb")
+        wsrc_sb = held.tile([P, D_BLOCKS, M], BF16, name="wsrc_sb")
+
+        nc.sync.dma_start(table_rows[0][:], table_blocks[:, 0 : S // P // 2, :])
+        nc.scalar.dma_start(table_rows[1][:], table_blocks[:, S // P // 2 : S // P, :])
+        nc.sync.dma_start(offsets[:], offs)
         nc.scalar.dma_start(w_sb[:], w)
+        nc.sync.dma_start(x_sb[:], x.rearrange("(c p) n -> p c n", p=P))
+        nc.scalar.dma_start(wsrc_sb[:], w_src.rearrange("(c p) m -> p c m", p=P))
+        nc.sync.dma_start(wdst_sb[:], w_dst.rearrange("(c p) m -> p c m", p=P))
+        bu_all = held.tile([P, ND], F32, name="bu_all")
+        nc.sync.dma_start(bu_all[:], bu.rearrange("d o -> (d o)").partition_broadcast(P))
 
         vec_rows = held.tile([P, P], F32, name="vec_rows")
         nc.vector.memset(vec_rows[:], 0.0)
         first_row = {}
         row = 0
-        for key, vec in (("b1", b1), ("b2", b2), ("bu", bu), ("gamma", gamma), ("beta", beta)):
+        for key, vec in (("b1", b1), ("b2", b2), ("gamma", gamma), ("beta", beta)):
             blocks = vec.shape[0] // P
             nc.gpsimd.dma_start(
                 vec_rows[row : row + blocks, :], vec.rearrange("(r c) o -> r (c o)", c=P)
             )
             first_row[key] = row
             row += blocks
-        wsrc_sb = held.tile([P, D_BLOCKS, M], BF16, name="wsrc_sb")
-        nc.gpsimd.dma_start(wsrc_sb[:], w_src.rearrange("(c p) m -> p c m", p=P))
+        for g in range(2):
+            nc.gpsimd.dma_start(w2_sb[g][:], w2_blocks[:, :, g * (F // 2) : (g + 1) * (F // 2)])
+        for g in range(2):
+            nc.gpsimd.dma_start(
+                wu_sb[g][:], wu_blocks[:, g * (F_BLOCKS // 2) : (g + 1) * (F_BLOCKS // 2), :]
+            )
 
-        w2_blocks = w2.rearrange("(c p) f -> p c f", p=P)
-        w2_sb = []
-        for g in range(4):
-            part = held.tile([P, M_BLOCKS, 4 * P], BF16, name=f"w2_sb{g}")
-            nc.sync.dma_start(part[:], w2_blocks[:, :, 4 * P * g : 4 * P * (g + 1)])
-            w2_sb.append(part)
-        wu_blocks = wu.rearrange("(b p) d -> p b d", p=P)
-        wu_sb = []
-        for g in range(4):
-            part = held.tile([P, 4, ND], BF16, name=f"wu_sb{g}")
-            nc.sync.dma_start(part[:], wu_blocks[:, 4 * g : 4 * (g + 1), :])
-            wu_sb.append(part)
-
-        ident_bf = held.tile([P, P], BF16, name="ident_bf")
-        make_identity(nc, ident_bf[:])
-        ident_f32 = held.tile([P, P], F32, name="ident_f32")
-        make_identity(nc, ident_f32[:])
-        mean_weights = held.tile([P, P], F32, name="mean_weights")
-        nc.vector.memset(mean_weights[:], 1.0 / ND)
         eps_col = held.tile([P, 1], F32, name="eps_col")
         nc.vector.memset(eps_col[:], EPS)
+
+        table_t = held.tile([P, S], BF16, name="table_t")
+        for g in range(4):
+            flipped = psum.tile([P, 8 * P], BF16, name="flipped", tag="bank")
+            for b in range(8):
+                nc.tensor.transpose(
+                    flipped[:, b * P : (b + 1) * P], table_rows[g // 2][:, 8 * (g % 2) + b, :], ident_bf[:]
+                )
+            target = table_t[:, 8 * P * g : 8 * P * (g + 1)]
+            if g % 2 == 0:
+                nc.vector.tensor_copy(target, flipped[:])
+            else:
+                nc.scalar.copy(target, flipped[:])
+
+        x_t = held.tile([P, ND], BF16, name="x_t")
+        xt_ps = psum.tile([P, ND], BF16, name="xt_ps", tag="bank")
+        for c in range(D_BLOCKS):
+            nc.tensor.transpose(xt_ps[:, c * P : (c + 1) * P], x_sb[:, c, :], ident_bf[:])
+        nc.vector.tensor_copy(x_t[:], xt_ps[:])
 
         vec_ps = psum.tile([P, P], F32, name="vec_ps", tag="bank")
         nc.tensor.transpose(vec_ps[:], vec_rows[:], ident_f32[:])
@@ -107,19 +121,6 @@ def tile_proteindecoder_b_kernel(
         def slope_col(key, block):
             c = first_row[key] + block
             return slope_cols[:, c : c + 1]
-
-        table_t = held.tile([P, S], BF16, name="table_t")
-        for g in range(4):
-            flipped = psum.tile([P, 8 * P], BF16, name="flipped", tag="bank")
-            for b in range(8):
-                nc.tensor.transpose(
-                    flipped[:, b * P : (b + 1) * P], table_rows[g][:, b, :], ident_bf[:]
-                )
-            target = table_t[:, 8 * P * g : 8 * P * (g + 1)]
-            if g % 2 == 0:
-                nc.vector.tensor_copy(target, flipped[:])
-            else:
-                nc.scalar.copy(target, flipped[:])
 
         r_ps = psum.tile([P, M], F32, name="r_ps", tag="bank")
         q_ps = psum.tile([P, M], F32, name="q_ps", tag="bank")
@@ -156,10 +157,7 @@ def tile_proteindecoder_b_kernel(
                     start=True,
                     stop=True,
                 )
-                if mb % 2 == 0:
-                    nc.scalar.copy(edge_p[:, mb, :], e_ps[:])
-                else:
-                    nc.vector.tensor_copy(edge_p[:, mb, :], e_ps[:])
+                nc.scalar.copy(edge_p[:, mb, :], e_ps[:])
             edge.append(edge_p)
 
         hidden = [None] * PIECES
@@ -170,7 +168,8 @@ def tile_proteindecoder_b_kernel(
                 nodes = slice(mb * P + NODES * p, mb * P + NODES * (p + 1))
                 shape = [P, NODES // L, L, L]
                 node_terms = terms.tile([P, PIECE], F32, name="node_terms")
-                nc.gpsimd.tensor_tensor(
+                adder = nc.vector if p == 0 else nc.gpsimd
+                adder.tensor_tensor(
                     node_terms[:].rearrange("q (g i t) -> q g i t", i=L, t=L),
                     rb_sb[:, nodes].rearrange("q (g i) -> q g i", i=L).unsqueeze(3).to_broadcast(shape),
                     q_sb[:, nodes].rearrange("q (g t) -> q g t", t=L).unsqueeze(2).to_broadcast(shape),
@@ -183,6 +182,18 @@ def tile_proteindecoder_b_kernel(
                 )
 
         agg = held.tile([P, F_BLOCKS, P], BF16, name="agg")
+        HALF = ND // 2
+        u_ps = []
+
+        def update_stage(fb):
+            for half in range(2):
+                nc.tensor.matmul(
+                    u_ps[half][:],
+                    agg[:, fb, :],
+                    wu_sb[fb // 8][:, fb % 8, half * HALF : (half + 1) * HALF],
+                    start=(fb == 0),
+                    stop=(fb == F_BLOCKS - 1),
+                )
 
         def message_stage(p):
             for fb in range(F_BLOCKS):
@@ -190,7 +201,7 @@ def tile_proteindecoder_b_kernel(
                 for c in range(M_BLOCKS):
                     nc.tensor.matmul(
                         m_ps[:],
-                        w2_sb[fb // 4][:, c, (fb % 4) * P : (fb % 4 + 1) * P],
+                        w2_sb[fb // 8][:, c, (fb % 8) * P : (fb % 8 + 1) * P],
                         hidden[p][:, c, :],
                         start=(c == 0),
                         stop=(c == M_BLOCKS - 1),
@@ -210,65 +221,47 @@ def tile_proteindecoder_b_kernel(
                         AXIS.X,
                         ALU.add,
                     )
+                if p == PIECES - 1:
+                    update_stage(fb)
 
         hidden_stage(0)
         for p in range(PIECES):
             if p + 1 < PIECES:
                 hidden_stage(p + 1)
+            else:
+                for half in range(2):
+                    u_ps.append(psum.tile([P, HALF], F32, name=f"u_ps{half}", tag="bank"))
             message_stage(p)
 
-        y = held.tile([P, D_BLOCKS, P], F32, name="y")
-        mean_ps = psum.tile([P, P], F32, name="mean_ps", tag="bank")
-
-        def add_to_mean(db):
-            nc.tensor.matmul(
-                mean_ps[:], mean_weights[:], y[:, db, :], start=(db == 0), stop=(db == D_BLOCKS - 1)
-            )
-
-        for db in range(D_BLOCKS):
-            u_ps = psum.tile([P, P], F32, name="u_ps", tag="bank")
-            for fb in range(F_BLOCKS):
-                nc.tensor.matmul(
-                    u_ps[:],
-                    wu_sb[fb // 4][:, fb % 4, db * P : (db + 1) * P],
-                    agg[:, fb, :],
-                    start=(fb == 0),
-                    stop=(fb == F_BLOCKS - 1),
-                )
-            u_low = work.tile([P, P], F32, name="u_low")
-            nc.scalar.activation(
-                u_low[:], u_ps[:], FUNC.Identity, bias=slope_col("bu", db), scale=SLOPE
-            )
-            u_sb = work.tile([P, P], F32, name="u_sb")
-            nc.vector.scalar_tensor_tensor(
-                u_sb[:], u_ps[:], col("bu", db), u_low[:], ALU.add, ALU.max
-            )
-            nc.vector.tensor_tensor(y[:, db, :], u_sb[:], x_sb[:, db, :], ALU.add)
-            if db > 0:
-                add_to_mean(db - 1)
-        add_to_mean(D_BLOCKS - 1)
-
-        centred = held.tile([P, D_BLOCKS, P], F32, name="centred")
-        squares = held.tile([P, D_BLOCKS, P], F32, name="squares")
-        var_ps = psum.tile([P, P], F32, name="var_ps", tag="bank")
-        for db in range(D_BLOCKS):
-            nc.vector.tensor_tensor(centred[:, db, :], y[:, db, :], mean_ps[:], ALU.subtract)
-            nc.scalar.activation(squares[:, db, :], centred[:, db, :], FUNC.Square)
-            nc.tensor.matmul(
-                var_ps[:], mean_weights[:], squares[:, db, :], start=(db == 0), stop=(db == D_BLOCKS - 1)
-            )
-        std = held.tile([P, P], F32, name="std")
-        nc.scalar.activation(std[:], var_ps[:], FUNC.Sqrt, bias=eps_col[:])
-        rstd = held.tile([P, P], F32, name="rstd")
+        y = held.tile([P, ND], F32, name="y")
+        stats = held.tile([P, 2, 6], F32, name="stats")
+        for half in range(2):
+            cols = slice(half * HALF, (half + 1) * HALF)
+            z = work.tile([P, HALF], F32, name="z")
+            nc.vector.tensor_tensor(z[:], u_ps[half][:], bu_all[:, cols], ALU.add)
+            u_sb = work.tile([P, HALF], F32, name="u_sb")
+            nc.vector.scalar_tensor_tensor(u_sb[:], z[:], SLOPE, z[:], ALU.mult, ALU.max)
+            nc.vector.tensor_tensor(y[:, cols], u_sb[:], x_t[:, cols], ALU.add)
+            nc.vector.bn_stats(stats[:, half, :], y[:, cols])
+        mean_var = held.tile([P, 2], F32, name="mean_var")
+        nc.vector.bn_aggr(mean_var[:], stats[:].rearrange("q a b -> q (a b)"))
+        std = held.tile([P, 1], F32, name="std")
+        nc.scalar.activation(std[:], mean_var[:, 1:2], FUNC.Sqrt, bias=eps_col[:])
+        rstd = held.tile([P, 1], F32, name="rstd")
         nc.vector.reciprocal(rstd[:], std[:])
 
-        out_blocks = out.rearrange("(c p) n -> p c n", p=P)
+        normal = held.tile([P, ND], F32, name="normal")
         result = held.tile([P, D_BLOCKS, P], F32, name="result")
+        out_blocks = out.rearrange("(c p) n -> p c n", p=P)
         for db in range(D_BLOCKS):
-            scaled = work.tile([P, P], F32, name="scaled")
-            nc.vector.scalar_tensor_tensor(
-                scaled[:], centred[:, db, :], col("gamma", db), rstd[:], ALU.mult, ALU.mult
+            cols = slice(db * P, (db + 1) * P)
+            nc.vector.tensor_scalar(
+                normal[:, cols], y[:, cols], mean_var[:, 0:1], rstd[:], ALU.subtract, ALU.mult
             )
-            nc.scalar.activation(result[:, db, :], scaled[:], FUNC.Identity, bias=col("beta", db))
+            turned = psum.tile([P, P], F32, name="turned", tag="bank")
+            nc.tensor.transpose(turned[:], normal[:, cols], ident_f32[:])
+            nc.scalar.activation(
+                result[:, db, :], turned[:], FUNC.Identity, bias=col("beta", db), scale=col("gamma", db)
+            )
             if db % 4 == 3:
                 nc.sync.dma_start(out_blocks[:, db - 3 : db + 1, :], result[:, db - 3 : db + 1, :])

@@ -176,7 +176,7 @@ def tile_proteindecoder_b_kernel(
                     ALU.add,
                 )
                 pre = work.tile([P, PIECE], F32, name="pre")
-                nc.vector.tensor_tensor(pre[:], edge[p][:, mb, :], node_terms[:], ALU.add)
+                adder.tensor_tensor(pre[:], edge[p][:, mb, :], node_terms[:], ALU.add)
                 nc.vector.scalar_tensor_tensor(
                     hidden[p][:, mb, :], pre[:], SLOPE, pre[:], ALU.mult, ALU.max
                 )
@@ -214,12 +214,14 @@ def tile_proteindecoder_b_kernel(
                 nc.vector.scalar_tensor_tensor(
                     msg[:], m_ps[:], col("b2", fb), low[:], ALU.add, ALU.max
                 )
+                senders = msg[:].rearrange("q (n t) -> q n t", t=L)
+                pairs = work.tile([P, NODES, L // 2], F32, name="pairs")
+                nc.gpsimd.tensor_tensor(
+                    pairs[:], senders[:, :, 0 : L // 2], senders[:, :, L // 2 : L], ALU.add
+                )
                 with nc.allow_low_precision(reason="summed in float32, rounded once to bfloat16"):
                     nc.vector.tensor_reduce(
-                        agg[:, fb, NODES * p : NODES * (p + 1)],
-                        msg[:].rearrange("q (n t) -> q n t", t=L),
-                        AXIS.X,
-                        ALU.add,
+                        agg[:, fb, NODES * p : NODES * (p + 1)], pairs[:], AXIS.X, ALU.add
                     )
                 if p == PIECES - 1:
                     update_stage(fb)

@@ -36,7 +36,7 @@ def tile_proteindecoder_b_kernel(
     nc = tc.nc
     with ExitStack() as ctx:
         held = ctx.enter_context(tc.tile_pool(name="held", bufs=1))
-        work = ctx.enter_context(tc.tile_pool(name="work", bufs=3))
+        work = ctx.enter_context(tc.tile_pool(name="work", bufs=4))
         terms = ctx.enter_context(tc.tile_pool(name="terms", bufs=4))
         psum = ctx.enter_context(tc.psum_pool(name="psum", bufs=8))
 
@@ -87,6 +87,8 @@ def tile_proteindecoder_b_kernel(
 
         eps_col = held.tile([P, 1], F32, name="eps_col")
         nc.vector.memset(eps_col[:], EPS)
+        warm_up = held.tile([P, 1], F32, name="warm_up")
+        nc.scalar.activation(warm_up[:], eps_col[:], FUNC.Sqrt)
 
         table_t = held.tile([P, S], BF16, name="table_t")
         for g in range(4):
@@ -100,12 +102,6 @@ def tile_proteindecoder_b_kernel(
                 nc.vector.tensor_copy(target, flipped[:])
             else:
                 nc.scalar.copy(target, flipped[:])
-
-        x_t = held.tile([P, ND], BF16, name="x_t")
-        xt_ps = psum.tile([P, ND], BF16, name="xt_ps", tag="bank")
-        for c in range(D_BLOCKS):
-            nc.tensor.transpose(xt_ps[:, c * P : (c + 1) * P], x_sb[:, c, :], ident_bf[:])
-        nc.vector.tensor_copy(x_t[:], xt_ps[:])
 
         vec_ps = psum.tile([P, P], F32, name="vec_ps", tag="bank")
         nc.tensor.transpose(vec_ps[:], vec_rows[:], ident_f32[:])
@@ -160,80 +156,110 @@ def tile_proteindecoder_b_kernel(
                 nc.scalar.copy(edge_p[:, mb, :], e_ps[:])
             edge.append(edge_p)
 
-        hidden = [None] * PIECES
+        PER_BLOCK = F_BLOCKS // M_BLOCKS
+        assert PIECES - 1 == PER_BLOCK - 1
+        hidden = [held.tile([P, M_BLOCKS, PIECE], BF16, name=f"hidden{p}") for p in range(PIECES)]
+        pre_of = {}
 
-        def hidden_stage(p):
-            hidden[p] = held.tile([P, M_BLOCKS, PIECE], BF16, name=f"hidden{p}")
-            for mb in range(M_BLOCKS):
-                nodes = slice(mb * P + NODES * p, mb * P + NODES * (p + 1))
-                shape = [P, NODES // L, L, L]
-                node_terms = terms.tile([P, PIECE], F32, name="node_terms")
-                adder = nc.vector if p == 0 else nc.gpsimd
-                adder.tensor_tensor(
-                    node_terms[:].rearrange("q (g i t) -> q g i t", i=L, t=L),
-                    rb_sb[:, nodes].rearrange("q (g i) -> q g i", i=L).unsqueeze(3).to_broadcast(shape),
-                    q_sb[:, nodes].rearrange("q (g t) -> q g t", t=L).unsqueeze(2).to_broadcast(shape),
-                    ALU.add,
-                )
-                pre = work.tile([P, PIECE], F32, name="pre")
-                adder.tensor_tensor(pre[:], edge[p][:, mb, :], node_terms[:], ALU.add)
-                nc.vector.scalar_tensor_tensor(
-                    hidden[p][:, mb, :], pre[:], SLOPE, pre[:], ALU.mult, ALU.max
-                )
+        def hidden_sums(p, mb):
+            nodes = slice(mb * P + NODES * p, mb * P + NODES * (p + 1))
+            shape = [P, NODES // L, L, L]
+            node_terms = terms.tile([P, PIECE], F32, name="node_terms")
+            adder = nc.vector if p == 0 else nc.gpsimd
+            adder.tensor_tensor(
+                node_terms[:].rearrange("q (g i t) -> q g i t", i=L, t=L),
+                rb_sb[:, nodes].rearrange("q (g i) -> q g i", i=L).unsqueeze(3).to_broadcast(shape),
+                q_sb[:, nodes].rearrange("q (g t) -> q g t", t=L).unsqueeze(2).to_broadcast(shape),
+                ALU.add,
+            )
+            pre = work.tile([P, PIECE], F32, name="pre")
+            adder.tensor_tensor(pre[:], edge[p][:, mb, :], node_terms[:], ALU.add)
+            pre_of[(p, mb)] = pre
+
+        def hidden_relu(p, mb):
+            pre = pre_of[(p, mb)]
+            nc.vector.scalar_tensor_tensor(
+                hidden[p][:, mb, :], pre[:], SLOPE, pre[:], ALU.mult, ALU.max
+            )
 
         agg = held.tile([P, F_BLOCKS, P], BF16, name="agg")
         HALF = ND // 2
         u_ps = []
+        summands = {}
 
-        def update_stage(fb):
-            for half in range(2):
+        def is_parked(p, fb):
+            return p < PIECES - 1 and fb % PER_BLOCK == PER_BLOCK - 1
+
+        def messages(p, fb):
+            m_ps = psum.tile([P, PIECE], F32, name="m_ps", tag="bank")
+            for c in range(M_BLOCKS):
                 nc.tensor.matmul(
-                    u_ps[half][:],
-                    agg[:, fb, :],
-                    wu_sb[fb // 8][:, fb % 8, half * HALF : (half + 1) * HALF],
-                    start=(fb == 0),
-                    stop=(fb == F_BLOCKS - 1),
+                    m_ps[:],
+                    w2_sb[fb // 8][:, c, (fb % 8) * P : (fb % 8 + 1) * P],
+                    hidden[p][:, c, :],
+                    start=(c == 0),
+                    stop=(c == M_BLOCKS - 1),
                 )
-
-        def message_stage(p):
-            for fb in range(F_BLOCKS):
-                m_ps = psum.tile([P, PIECE], F32, name="m_ps", tag="bank")
-                for c in range(M_BLOCKS):
-                    nc.tensor.matmul(
-                        m_ps[:],
-                        w2_sb[fb // 8][:, c, (fb % 8) * P : (fb % 8 + 1) * P],
-                        hidden[p][:, c, :],
-                        start=(c == 0),
-                        stop=(c == M_BLOCKS - 1),
-                    )
-                low = work.tile([P, PIECE], F32, name="low")
-                nc.scalar.activation(
-                    low[:], m_ps[:], FUNC.Identity, bias=slope_col("b2", fb), scale=SLOPE
-                )
-                msg = work.tile([P, PIECE], F32, name="msg")
-                nc.vector.scalar_tensor_tensor(
-                    msg[:], m_ps[:], col("b2", fb), low[:], ALU.add, ALU.max
-                )
-                senders = msg[:].rearrange("q (n t) -> q n t", t=L)
-                pairs = work.tile([P, NODES, L // 2], F32, name="pairs")
-                nc.gpsimd.tensor_tensor(
-                    pairs[:], senders[:, :, 0 : L // 2], senders[:, :, L // 2 : L], ALU.add
-                )
-                with nc.allow_low_precision(reason="summed in float32, rounded once to bfloat16"):
-                    nc.vector.tensor_reduce(
-                        agg[:, fb, NODES * p : NODES * (p + 1)], pairs[:], AXIS.X, ALU.add
-                    )
-                if p == PIECES - 1:
-                    update_stage(fb)
-
-        hidden_stage(0)
-        for p in range(PIECES):
-            if p + 1 < PIECES:
-                hidden_stage(p + 1)
+            low = work.tile([P, PIECE], F32, name="low")
+            nc.scalar.activation(
+                low[:], m_ps[:], FUNC.Identity, bias=slope_col("b2", fb), scale=SLOPE
+            )
+            if is_parked(p, fb):
+                msg = held.tile([P, PIECE], F32, name=f"parked{p}_{fb}")
             else:
+                msg = work.tile([P, PIECE], F32, name="msg")
+            nc.vector.scalar_tensor_tensor(
+                msg[:], m_ps[:], col("b2", fb), low[:], ALU.add, ALU.max
+            )
+            senders = msg[:].rearrange("q (n t) -> q n t", t=L)
+            summands[(p, fb)] = senders
+
+        def aggregate(p, fb):
+            with nc.allow_low_precision(reason="summed in float32, rounded once to bfloat16"):
+                nc.vector.tensor_reduce(
+                    agg[:, fb, NODES * p : NODES * (p + 1)], summands[(p, fb)], AXIS.X, ALU.add
+                )
+            if p == PIECES - 1:
                 for half in range(2):
-                    u_ps.append(psum.tile([P, HALF], F32, name=f"u_ps{half}", tag="bank"))
-            message_stage(p)
+                    nc.tensor.matmul(
+                        u_ps[half][:],
+                        agg[:, fb, :],
+                        wu_sb[fb // 8][:, fb % 8, half * HALF : (half + 1) * HALF],
+                        start=(fb == 0),
+                        stop=(fb == F_BLOCKS - 1),
+                    )
+
+        x_t = held.tile([P, ND], BF16, name="x_t")
+
+        def turn_x():
+            xt_ps = psum.tile([P, ND], BF16, name="xt_ps", tag="bank")
+            for c in range(D_BLOCKS):
+                nc.tensor.transpose(xt_ps[:, c * P : (c + 1) * P], x_sb[:, c, :], ident_bf[:])
+            nc.scalar.copy(x_t[:], xt_ps[:])
+
+        for mb in range(M_BLOCKS):
+            hidden_sums(0, mb)
+            hidden_relu(0, mb)
+
+        STEPS = PIECES * F_BLOCKS
+        LAG = 1
+        for step in range(STEPS + LAG):
+            if step < STEPS:
+                p, fb = divmod(step, F_BLOCKS)
+                if p == 1 and fb == 0:
+                    turn_x()
+                if p == PIECES - 1 and fb == 0:
+                    for half in range(2):
+                        u_ps.append(psum.tile([P, HALF], F32, name=f"u_ps{half}", tag="bank"))
+                messages(p, fb)
+                if p + 1 < PIECES and fb % PER_BLOCK == 0:
+                    hidden_sums(p + 1, fb // PER_BLOCK)
+                if p + 1 < PIECES and fb % PER_BLOCK == PER_BLOCK - 1:
+                    hidden_relu(p + 1, fb // PER_BLOCK)
+                if p == PIECES - 1 and fb % PER_BLOCK < PER_BLOCK - 1:
+                    aggregate(fb % PER_BLOCK, fb - fb % PER_BLOCK + PER_BLOCK - 1)
+            if step >= LAG and not is_parked(*divmod(step - LAG, F_BLOCKS)):
+                aggregate(*divmod(step - LAG, F_BLOCKS))
 
         y = held.tile([P, ND], F32, name="y")
         stats = held.tile([P, 2, 6], F32, name="stats")
@@ -253,17 +279,24 @@ def tile_proteindecoder_b_kernel(
         nc.vector.reciprocal(rstd[:], std[:])
 
         normal = held.tile([P, ND], F32, name="normal")
-        result = held.tile([P, D_BLOCKS, P], F32, name="result")
-        out_blocks = out.rearrange("(c p) n -> p c n", p=P)
-        for db in range(D_BLOCKS):
-            cols = slice(db * P, (db + 1) * P)
+        for half in range(2):
+            cols = slice(half * HALF, (half + 1) * HALF)
             nc.vector.tensor_scalar(
                 normal[:, cols], y[:, cols], mean_var[:, 0:1], rstd[:], ALU.subtract, ALU.mult
             )
+
+        result = held.tile([P, D_BLOCKS, P], F32, name="result")
+        out_blocks = out.rearrange("(c p) n -> p c n", p=P)
+        for db in range(D_BLOCKS):
             turned = psum.tile([P, P], F32, name="turned", tag="bank")
-            nc.tensor.transpose(turned[:], normal[:, cols], ident_f32[:])
-            nc.scalar.activation(
-                result[:, db, :], turned[:], FUNC.Identity, bias=col("beta", db), scale=col("gamma", db)
-            )
-            if db % 4 == 3:
-                nc.sync.dma_start(out_blocks[:, db - 3 : db + 1, :], result[:, db - 3 : db + 1, :])
+            nc.tensor.transpose(turned[:], normal[:, db * P : (db + 1) * P], ident_f32[:])
+            if db % 2 == 0:
+                nc.scalar.activation(
+                    result[:, db, :], turned[:], FUNC.Identity, bias=col("beta", db), scale=col("gamma", db)
+                )
+            else:
+                nc.vector.tensor_scalar(
+                    result[:, db, :], turned[:], col("gamma", db), col("beta", db), ALU.mult, ALU.add
+                )
+        nc.gpsimd.dma_start(out_blocks[:, 0 : D_BLOCKS // 2, :], result[:, 0 : D_BLOCKS // 2, :])
+        nc.sync.dma_start(out_blocks[:, D_BLOCKS // 2 :, :], result[:, D_BLOCKS // 2 :, :])

@@ -61,11 +61,13 @@ def tile_proteindecoder_b_kernel(
         nc.scalar.dma_start(table_rows[1][:], table_blocks[:, S // P // 2 : S // P, :])
         nc.sync.dma_start(offsets[:], offs)
         nc.scalar.dma_start(w_sb[:], w)
-        nc.sync.dma_start(x_sb[:], x.rearrange("(c p) n -> p c n", p=P))
-        nc.scalar.dma_start(wsrc_sb[:], w_src.rearrange("(c p) m -> p c m", p=P))
-        nc.sync.dma_start(wdst_sb[:], w_dst.rearrange("(c p) m -> p c m", p=P))
+        nc.sync.dma_start(x_sb[:], x.rearrange("(p c) n -> p c n", p=P))
+        nc.scalar.dma_start(wsrc_sb[:], w_src.rearrange("(p c) m -> p c m", p=P))
+        nc.sync.dma_start(wdst_sb[:], w_dst.rearrange("(p c) m -> p c m", p=P))
         bu_all = held.tile([P, ND], F32, name="bu_all")
         nc.sync.dma_start(bu_all[:], bu.rearrange("d o -> (d o)").partition_broadcast(P))
+        x_blocks = held.tile([P, D_BLOCKS, P], BF16, name="x_blocks")
+        nc.sync.dma_start(x_blocks[:], x.rearrange("(c p) n -> p c n", p=P))
 
         vec_rows = held.tile([P, P], F32, name="vec_rows")
         nc.vector.memset(vec_rows[:], 0.0)
@@ -234,7 +236,7 @@ def tile_proteindecoder_b_kernel(
         def turn_x():
             xt_ps = psum.tile([P, ND], BF16, name="xt_ps", tag="bank")
             for c in range(D_BLOCKS):
-                nc.tensor.transpose(xt_ps[:, c * P : (c + 1) * P], x_sb[:, c, :], ident_bf[:])
+                nc.tensor.transpose(xt_ps[:, c * P : (c + 1) * P], x_blocks[:, c, :], ident_bf[:])
             nc.scalar.copy(x_t[:], xt_ps[:])
 
         for mb in range(M_BLOCKS):
@@ -242,7 +244,7 @@ def tile_proteindecoder_b_kernel(
             hidden_relu(0, mb)
 
         STEPS = PIECES * F_BLOCKS
-        LAG = 1
+        LAG = 2
         for step in range(STEPS + LAG):
             if step < STEPS:
                 p, fb = divmod(step, F_BLOCKS)
@@ -298,5 +300,5 @@ def tile_proteindecoder_b_kernel(
                 nc.vector.tensor_scalar(
                     result[:, db, :], turned[:], col("gamma", db), col("beta", db), ALU.mult, ALU.add
                 )
-        nc.gpsimd.dma_start(out_blocks[:, 0 : D_BLOCKS // 2, :], result[:, 0 : D_BLOCKS // 2, :])
-        nc.sync.dma_start(out_blocks[:, D_BLOCKS // 2 :, :], result[:, D_BLOCKS // 2 :, :])
+            if db % 4 == 3:
+                nc.sync.dma_start(out_blocks[:, db - 3 : db + 1, :], result[:, db - 3 : db + 1, :])

@@ -45,10 +45,12 @@ def tile_proteindecoder_b_kernel(
         ident_f32 = held.tile([P, P], F32, name="ident_f32")
         make_identity(nc, ident_f32[:])
 
-        table_blocks = table.rearrange("(b p) k -> p b k", p=P)
+        GROUPS = 4
+        RUN = S // GROUPS // P
+        table_groups = table.rearrange("(g p j) k -> p g (j k)", p=P, j=RUN)
         w2_blocks = w2.rearrange("(c p) f -> p c f", p=P)
         wu_blocks = wu.rearrange("(b p) d -> p b d", p=P)
-        table_rows = [held.tile([P, S // P // 2, P], BF16, name=f"table_rows{g}") for g in range(2)]
+        table_rows = [held.tile([P, GROUPS // 2, RUN * P], BF16, name=f"table_rows{g}") for g in range(2)]
         w2_sb = [held.tile([P, M_BLOCKS, F // 2], BF16, name=f"w2_sb{g}") for g in range(2)]
         wu_sb = [held.tile([P, F_BLOCKS // 2, ND], BF16, name=f"wu_sb{g}") for g in range(2)]
         offsets = held.tile([P, N // 16], U16, name="offsets")
@@ -57,8 +59,8 @@ def tile_proteindecoder_b_kernel(
         wdst_sb = held.tile([P, D_BLOCKS, M], BF16, name="wdst_sb")
         wsrc_sb = held.tile([P, D_BLOCKS, M], BF16, name="wsrc_sb")
 
-        nc.sync.dma_start(table_rows[0][:], table_blocks[:, 0 : S // P // 2, :])
-        nc.scalar.dma_start(table_rows[1][:], table_blocks[:, S // P // 2 : S // P, :])
+        nc.sync.dma_start(table_rows[0][:], table_groups[:, 0 : GROUPS // 2, :])
+        nc.scalar.dma_start(table_rows[1][:], table_groups[:, GROUPS // 2 : GROUPS, :])
         nc.sync.dma_start(offsets[:], offs)
         nc.scalar.dma_start(w_sb[:], w)
         nc.sync.dma_start(x_sb[:], x.rearrange("(p c) n -> p c n", p=P))
@@ -93,17 +95,20 @@ def tile_proteindecoder_b_kernel(
         nc.scalar.activation(warm_up[:], eps_col[:], FUNC.Sqrt)
 
         table_t = held.tile([P, S], BF16, name="table_t")
-        for g in range(4):
-            flipped = psum.tile([P, 8 * P], BF16, name="flipped", tag="bank")
-            for b in range(8):
+        for g in range(GROUPS):
+            flipped = psum.tile([P, RUN * P], BF16, name="flipped", tag="bank")
+            for j in range(RUN):
                 nc.tensor.transpose(
-                    flipped[:, b * P : (b + 1) * P], table_rows[g // 2][:, 8 * (g % 2) + b, :], ident_bf[:]
+                    flipped[:, j * P : (j + 1) * P],
+                    table_rows[g // 2][:, g % 2, j * P : (j + 1) * P],
+                    ident_bf[:],
                 )
-            target = table_t[:, 8 * P * g : 8 * P * (g + 1)]
+            target = table_t[:, RUN * P * g : RUN * P * (g + 1)].rearrange("k (p j) -> k p j", j=RUN)
+            crosswise = flipped[:].rearrange("k (j p) -> k p j", p=P)
             if g % 2 == 0:
-                nc.vector.tensor_copy(target, flipped[:])
+                nc.vector.tensor_copy(target, crosswise)
             else:
-                nc.scalar.copy(target, flipped[:])
+                nc.scalar.copy(target, crosswise)
 
         vec_ps = psum.tile([P, P], F32, name="vec_ps", tag="bank")
         nc.tensor.transpose(vec_ps[:], vec_rows[:], ident_f32[:])

@@ -226,15 +226,6 @@ def tile_proteindecoder_b_kernel(
                 nc.vector.tensor_reduce(
                     agg[:, fb, NODES * p : NODES * (p + 1)], summands[(p, fb)], AXIS.X, ALU.add
                 )
-            if p == PIECES - 1:
-                for half in range(2):
-                    nc.tensor.matmul(
-                        u_ps[half][:],
-                        agg[:, fb, :],
-                        wu_sb[fb // 8][:, fb % 8, half * HALF : (half + 1) * HALF],
-                        start=(fb == 0),
-                        stop=(fb == F_BLOCKS - 1),
-                    )
 
         x_t = held.tile([P, ND], BF16, name="x_t")
 
@@ -255,9 +246,6 @@ def tile_proteindecoder_b_kernel(
                 p, fb = divmod(step, F_BLOCKS)
                 if p == 1 and fb == 0:
                     turn_x()
-                if p == PIECES - 1 and fb == 0:
-                    for half in range(2):
-                        u_ps.append(psum.tile([P, HALF], F32, name=f"u_ps{half}", tag="bank"))
                 messages(p, fb)
                 if p + 1 < PIECES and fb % PER_BLOCK == 0:
                     hidden_sums(p + 1, fb // PER_BLOCK)
@@ -267,6 +255,18 @@ def tile_proteindecoder_b_kernel(
                     aggregate(fb % PER_BLOCK, fb - fb % PER_BLOCK + PER_BLOCK - 1)
             if step >= LAG and not is_parked(*divmod(step - LAG, F_BLOCKS)):
                 aggregate(*divmod(step - LAG, F_BLOCKS))
+
+        for half in range(2):
+            u_ps.append(psum.tile([P, HALF], F32, name=f"u_ps{half}", tag="bank"))
+        for fb in range(F_BLOCKS):
+            for half in range(2):
+                nc.tensor.matmul(
+                    u_ps[half][:],
+                    agg[:, fb, :],
+                    wu_sb[fb // 8][:, fb % 8, half * HALF : (half + 1) * HALF],
+                    start=(fb == 0),
+                    stop=(fb == F_BLOCKS - 1),
+                )
 
         y = held.tile([P, ND], F32, name="y")
         stats = held.tile([P, 2, 6], F32, name="stats")

@@ -50,7 +50,7 @@ def tile_proteindecoder_b_kernel(
         table_groups = table.rearrange("(g p j) k -> p g (j k)", p=P, j=RUN)
         w2_blocks = w2.rearrange("(c p) f -> p c f", p=P)
         wu_blocks = wu.rearrange("(b p) d -> p b d", p=P)
-        table_rows = [held.tile([P, GROUPS // 2, RUN * P], BF16, name=f"table_rows{g}") for g in range(2)]
+        table_rows = [held.tile([P, RUN * P], BF16, name=f"table_rows{g}") for g in range(GROUPS)]
         w2_sb = [held.tile([P, M_BLOCKS, F // 2], BF16, name=f"w2_sb{g}") for g in range(2)]
         wu_sb = [held.tile([P, F_BLOCKS // 2, ND], BF16, name=f"wu_sb{g}") for g in range(2)]
         offsets = held.tile([P, N // 16], U16, name="offsets")
@@ -59,8 +59,9 @@ def tile_proteindecoder_b_kernel(
         wdst_sb = held.tile([P, D_BLOCKS, M], BF16, name="wdst_sb")
         wsrc_sb = held.tile([P, D_BLOCKS, M], BF16, name="wsrc_sb")
 
-        nc.sync.dma_start(table_rows[0][:], table_groups[:, 0 : GROUPS // 2, :])
-        nc.scalar.dma_start(table_rows[1][:], table_groups[:, GROUPS // 2 : GROUPS, :])
+        for g in range(GROUPS):
+            queue = nc.sync if g % 2 == 0 else nc.scalar
+            queue.dma_start(table_rows[g][:], table_groups[:, g, :])
         nc.sync.dma_start(offsets[:], offs)
         nc.scalar.dma_start(w_sb[:], w)
         nc.sync.dma_start(x_sb[:], x.rearrange("(p c) n -> p c n", p=P))
@@ -100,7 +101,7 @@ def tile_proteindecoder_b_kernel(
             for j in range(RUN):
                 nc.tensor.transpose(
                     flipped[:, j * P : (j + 1) * P],
-                    table_rows[g // 2][:, g % 2, j * P : (j + 1) * P],
+                    table_rows[g][:, j * P : (j + 1) * P],
                     ident_bf[:],
                 )
             target = table_t[:, RUN * P * g : RUN * P * (g + 1)].rearrange("k (p j) -> k p j", j=RUN)
@@ -109,6 +110,24 @@ def tile_proteindecoder_b_kernel(
                 nc.vector.tensor_copy(target, crosswise)
             else:
                 nc.scalar.copy(target, crosswise)
+
+        edge = []
+
+        def look_up(p):
+            edge_p = held.tile([P, M_BLOCKS, PIECE], F32, name=f"edge{p}")
+            for mb in range(M_BLOCKS):
+                e_ps = psum.tile([P, PIECE], F32, name="e_ps", tag="bank")
+                nc.tensor.matmul(
+                    e_ps[:],
+                    w_sb[:, mb * P : (mb + 1) * P],
+                    table_t[:].indirect(offsets[:, (PIECE // 16) * p : (PIECE // 16) * (p + 1)]),
+                    start=True,
+                    stop=True,
+                )
+                nc.scalar.copy(edge_p[:, mb, :], e_ps[:])
+            edge.append(edge_p)
+
+        look_up(0)
 
         vec_ps = psum.tile([P, P], F32, name="vec_ps", tag="bank")
         nc.tensor.transpose(vec_ps[:], vec_rows[:], ident_f32[:])
@@ -125,9 +144,9 @@ def tile_proteindecoder_b_kernel(
             c = first_row[key] + block
             return slope_cols[:, c : c + 1]
 
-        r_ps = psum.tile([P, M], F32, name="r_ps", tag="bank")
         q_ps = psum.tile([P, M], F32, name="q_ps", tag="bank")
-        for ps, weights in ((r_ps, wdst_sb), (q_ps, wsrc_sb)):
+        r_ps = psum.tile([P, M], F32, name="r_ps", tag="bank")
+        for ps, weights in ((q_ps, wsrc_sb), (r_ps, wdst_sb)):
             for mb in range(M_BLOCKS):
                 for c in range(D_BLOCKS):
                     nc.tensor.matmul(
@@ -137,31 +156,19 @@ def tile_proteindecoder_b_kernel(
                         start=(c == 0),
                         stop=(c == D_BLOCKS - 1),
                     )
-        rb_sb = held.tile([P, M], F32, name="rb_sb")
+        qb_sb = held.tile([P, M], F32, name="qb_sb")
         for mb in range(M_BLOCKS):
             nc.scalar.activation(
-                rb_sb[:, mb * P : (mb + 1) * P],
-                r_ps[:, mb * P : (mb + 1) * P],
+                qb_sb[:, mb * P : (mb + 1) * P],
+                q_ps[:, mb * P : (mb + 1) * P],
                 FUNC.Identity,
                 bias=col("b1", mb),
             )
-        q_sb = held.tile([P, M], F32, name="q_sb")
-        nc.vector.tensor_copy(q_sb[:], q_ps[:])
+        r_sb = held.tile([P, M], F32, name="r_sb")
+        nc.vector.tensor_copy(r_sb[:], r_ps[:])
 
-        edge = []
-        for p in range(PIECES):
-            edge_p = held.tile([P, M_BLOCKS, PIECE], F32, name=f"edge{p}")
-            for mb in range(M_BLOCKS):
-                e_ps = psum.tile([P, PIECE], F32, name="e_ps", tag="bank")
-                nc.tensor.matmul(
-                    e_ps[:],
-                    w_sb[:, mb * P : (mb + 1) * P],
-                    table_t[:].indirect(offsets[:, (PIECE // 16) * p : (PIECE // 16) * (p + 1)]),
-                    start=True,
-                    stop=True,
-                )
-                nc.scalar.copy(edge_p[:, mb, :], e_ps[:])
-            edge.append(edge_p)
+        for p in range(1, PIECES):
+            look_up(p)
 
         PER_BLOCK = F_BLOCKS // M_BLOCKS
         assert PIECES - 1 == PER_BLOCK - 1
@@ -171,16 +178,22 @@ def tile_proteindecoder_b_kernel(
         def hidden_sums(p, mb):
             nodes = slice(mb * P + NODES * p, mb * P + NODES * (p + 1))
             shape = [P, NODES // L, L, L]
-            node_terms = terms.tile([P, PIECE], F32, name="node_terms")
+            by_pair = "q (g i t) -> q g i t"
             adder = nc.vector if p == 0 else nc.gpsimd
+            with_sender = terms.tile([P, PIECE], F32, name="with_sender")
             adder.tensor_tensor(
-                node_terms[:].rearrange("q (g i t) -> q g i t", i=L, t=L),
-                rb_sb[:, nodes].rearrange("q (g i) -> q g i", i=L).unsqueeze(3).to_broadcast(shape),
-                q_sb[:, nodes].rearrange("q (g t) -> q g t", t=L).unsqueeze(2).to_broadcast(shape),
+                with_sender[:].rearrange(by_pair, i=L, t=L),
+                edge[p][:, mb, :].rearrange(by_pair, i=L, t=L),
+                qb_sb[:, nodes].rearrange("q (g t) -> q g t", t=L).unsqueeze(2).to_broadcast(shape),
                 ALU.add,
             )
             pre = work.tile([P, PIECE], F32, name="pre")
-            adder.tensor_tensor(pre[:], edge[p][:, mb, :], node_terms[:], ALU.add)
+            adder.tensor_tensor(
+                pre[:].rearrange(by_pair, i=L, t=L),
+                with_sender[:].rearrange(by_pair, i=L, t=L),
+                r_sb[:, nodes].rearrange("q (g i) -> q g i", i=L).unsqueeze(3).to_broadcast(shape),
+                ALU.add,
+            )
             pre_of[(p, mb)] = pre
 
         def hidden_relu(p, mb):

@@ -64,6 +64,17 @@ def tile_proteindecoder_b_kernel(
             queue.dma_start(table_rows[g][:], table_groups[:, g, :])
         nc.sync.dma_start(offsets[:], offs)
         nc.scalar.dma_start(w_sb[:], w)
+        vec_rows = held.tile([P, P], F32, name="vec_rows")
+        nc.vector.memset(vec_rows[:], 0.0)
+        first_row = {}
+        row = 0
+        for key, vec in (("b1", b1), ("b2", b2), ("gamma", gamma), ("beta", beta)):
+            blocks = vec.shape[0] // P
+            nc.sync.dma_start(
+                vec_rows[row : row + blocks, :], vec.rearrange("(r c) o -> r (c o)", c=P)
+            )
+            first_row[key] = row
+            row += blocks
         nc.sync.dma_start(x_sb[:], x.rearrange("(p c) n -> p c n", p=P))
         nc.scalar.dma_start(wsrc_sb[:], w_src.rearrange("(p c) m -> p c m", p=P))
         nc.sync.dma_start(wdst_sb[:], w_dst.rearrange("(p c) m -> p c m", p=P))
@@ -72,17 +83,6 @@ def tile_proteindecoder_b_kernel(
         x_blocks = held.tile([P, D_BLOCKS, P], BF16, name="x_blocks")
         nc.sync.dma_start(x_blocks[:], x.rearrange("(c p) n -> p c n", p=P))
 
-        vec_rows = held.tile([P, P], F32, name="vec_rows")
-        nc.vector.memset(vec_rows[:], 0.0)
-        first_row = {}
-        row = 0
-        for key, vec in (("b1", b1), ("b2", b2), ("gamma", gamma), ("beta", beta)):
-            blocks = vec.shape[0] // P
-            nc.gpsimd.dma_start(
-                vec_rows[row : row + blocks, :], vec.rearrange("(r c) o -> r (c o)", c=P)
-            )
-            first_row[key] = row
-            row += blocks
         for g in range(2):
             nc.gpsimd.dma_start(w2_sb[g][:], w2_blocks[:, :, g * (F // 2) : (g + 1) * (F // 2)])
         for g in range(2):
@@ -135,6 +135,8 @@ def tile_proteindecoder_b_kernel(
         nc.vector.tensor_copy(vec_cols[:], vec_ps[:])
         slope_cols = held.tile([P, P], F32, name="slope_cols")
         nc.vector.tensor_scalar(slope_cols[:], vec_cols[:], SLOPE, None, ALU.mult)
+        steep_cols = held.tile([P, P], F32, name="steep_cols")
+        nc.vector.tensor_scalar(steep_cols[:], vec_cols[:], 1.0 - SLOPE, None, ALU.mult)
 
         def col(key, block):
             c = first_row[key] + block
@@ -143,6 +145,10 @@ def tile_proteindecoder_b_kernel(
         def slope_col(key, block):
             c = first_row[key] + block
             return slope_cols[:, c : c + 1]
+
+        def steep_col(key, block):
+            c = first_row[key] + block
+            return steep_cols[:, c : c + 1]
 
         q_ps = psum.tile([P, M], F32, name="q_ps", tag="bank")
         r_ps = psum.tile([P, M], F32, name="r_ps", tag="bank")
@@ -171,7 +177,6 @@ def tile_proteindecoder_b_kernel(
             look_up(p)
 
         PER_BLOCK = F_BLOCKS // M_BLOCKS
-        assert PIECES - 1 == PER_BLOCK - 1
         hidden = [held.tile([P, M_BLOCKS, PIECE], BF16, name=f"hidden{p}") for p in range(PIECES)]
         pre_of = {}
 
@@ -207,8 +212,13 @@ def tile_proteindecoder_b_kernel(
         u_ps = []
         summands = {}
 
+        LATE = PIECES // 2
+
+        def without_vector(p, fb):
+            return p >= LATE and fb % 2 == 1
+
         def is_parked(p, fb):
-            return p < PIECES - 1 and fb % PER_BLOCK == PER_BLOCK - 1
+            return p < LATE and fb % PER_BLOCK == PER_BLOCK - 1
 
         def messages(p, fb):
             m_ps = psum.tile([P, PIECE], F32, name="m_ps", tag="bank")
@@ -228,9 +238,16 @@ def tile_proteindecoder_b_kernel(
                 msg = held.tile([P, PIECE], F32, name=f"parked{p}_{fb}")
             else:
                 msg = work.tile([P, PIECE], F32, name="msg")
-            nc.vector.scalar_tensor_tensor(
-                msg[:], m_ps[:], col("b2", fb), low[:], ALU.add, ALU.max
-            )
+            if without_vector(p, fb):
+                steep = work.tile([P, PIECE], F32, name="steep")
+                nc.scalar.activation(
+                    steep[:], m_ps[:], FUNC.Relu, bias=steep_col("b2", fb), scale=1.0 - SLOPE
+                )
+                nc.gpsimd.tensor_tensor(msg[:], steep[:], low[:], ALU.add)
+            else:
+                nc.vector.scalar_tensor_tensor(
+                    msg[:], m_ps[:], col("b2", fb), low[:], ALU.add, ALU.max
+                )
             senders = msg[:].rearrange("q (n t) -> q n t", t=L)
             summands[(p, fb)] = senders
 
@@ -264,15 +281,14 @@ def tile_proteindecoder_b_kernel(
                     hidden_sums(p + 1, fb // PER_BLOCK)
                 if p + 1 < PIECES and fb % PER_BLOCK == PER_BLOCK - 1:
                     hidden_relu(p + 1, fb // PER_BLOCK)
-                if p == PIECES - 1 and fb % PER_BLOCK < PER_BLOCK - 1:
-                    aggregate(fb % PER_BLOCK, fb - fb % PER_BLOCK + PER_BLOCK - 1)
+                if p >= LATE and is_parked(p - LATE, fb):
+                    aggregate(p - LATE, fb)
             if step >= LAG and not is_parked(*divmod(step - LAG, F_BLOCKS)):
                 aggregate(*divmod(step - LAG, F_BLOCKS))
 
         for half in range(2):
             u_ps.append(psum.tile([P, HALF], F32, name=f"u_ps{half}", tag="bank"))
-        for fb in range(F_BLOCKS):
-            for half in range(2):
+            for fb in range(F_BLOCKS):
                 nc.tensor.matmul(
                     u_ps[half][:],
                     agg[:, fb, :],
@@ -298,12 +314,15 @@ def tile_proteindecoder_b_kernel(
         rstd = held.tile([P, 1], F32, name="rstd")
         nc.vector.reciprocal(rstd[:], std[:])
 
+        shift = held.tile([P, 1], F32, name="shift")
+        nc.vector.scalar_tensor_tensor(shift[:], mean_var[:, 0:1], -1.0, rstd[:], ALU.mult, ALU.mult)
         normal = held.tile([P, ND], F32, name="normal")
-        for half in range(2):
-            cols = slice(half * HALF, (half + 1) * HALF)
-            nc.vector.tensor_scalar(
-                normal[:, cols], y[:, cols], mean_var[:, 0:1], rstd[:], ALU.subtract, ALU.mult
-            )
+        nc.vector.tensor_scalar(
+            normal[:, 0:HALF], y[:, 0:HALF], mean_var[:, 0:1], rstd[:], ALU.subtract, ALU.mult
+        )
+        nc.scalar.activation(
+            normal[:, HALF:ND], y[:, HALF:ND], FUNC.Identity, bias=shift[:], scale=rstd[:]
+        )
 
         result = held.tile([P, D_BLOCKS, P], F32, name="result")
         out_blocks = out.rearrange("(c p) n -> p c n", p=P)
@@ -318,5 +337,5 @@ def tile_proteindecoder_b_kernel(
                 nc.vector.tensor_scalar(
                     result[:, db, :], turned[:], col("gamma", db), col("beta", db), ALU.mult, ALU.add
                 )
-            if db % 4 == 3:
-                nc.sync.dma_start(out_blocks[:, db - 3 : db + 1, :], result[:, db - 3 : db + 1, :])
+            if db % 2 == 1:
+                nc.sync.dma_start(out_blocks[:, db - 1 : db + 1, :], result[:, db - 1 : db + 1, :])

@@ -60,10 +60,9 @@ def tile_proteindecoder_b_kernel(
         wsrc_sb = held.tile([P, D_BLOCKS, M], BF16, name="wsrc_sb")
 
         for g in range(GROUPS):
-            queue = nc.sync if g % 2 == 0 else nc.scalar
-            queue.dma_start(table_rows[g][:], table_groups[:, g, :])
+            nc.sync.dma_start(table_rows[g][:], table_groups[:, g, :])
         nc.sync.dma_start(offsets[:], offs)
-        nc.scalar.dma_start(w_sb[:], w)
+        nc.sync.dma_start(w_sb[:], w)
         vec_rows = held.tile([P, P], F32, name="vec_rows")
         nc.vector.memset(vec_rows[:], 0.0)
         first_row = {}
@@ -76,24 +75,24 @@ def tile_proteindecoder_b_kernel(
             first_row[key] = row
             row += blocks
         nc.sync.dma_start(x_sb[:], x.rearrange("(p c) n -> p c n", p=P))
-        nc.scalar.dma_start(wsrc_sb[:], w_src.rearrange("(p c) m -> p c m", p=P))
+        nc.sync.dma_start(wsrc_sb[:], w_src.rearrange("(p c) m -> p c m", p=P))
         nc.sync.dma_start(wdst_sb[:], w_dst.rearrange("(p c) m -> p c m", p=P))
+        for g in range(2):
+            nc.sync.dma_start(w2_sb[g][:], w2_blocks[:, :, g * (F // 2) : (g + 1) * (F // 2)])
         bu_all = held.tile([P, ND], F32, name="bu_all")
         nc.sync.dma_start(bu_all[:], bu.rearrange("d o -> (d o)").partition_broadcast(P))
         x_blocks = held.tile([P, D_BLOCKS, P], BF16, name="x_blocks")
         nc.sync.dma_start(x_blocks[:], x.rearrange("(c p) n -> p c n", p=P))
 
         for g in range(2):
-            nc.gpsimd.dma_start(w2_sb[g][:], w2_blocks[:, :, g * (F // 2) : (g + 1) * (F // 2)])
-        for g in range(2):
-            nc.gpsimd.dma_start(
+            nc.sync.dma_start(
                 wu_sb[g][:], wu_blocks[:, g * (F_BLOCKS // 2) : (g + 1) * (F_BLOCKS // 2), :]
             )
 
         eps_col = held.tile([P, 1], F32, name="eps_col")
         nc.vector.memset(eps_col[:], EPS)
         warm_up = held.tile([P, 1], F32, name="warm_up")
-        nc.scalar.activation(warm_up[:], eps_col[:], FUNC.Sqrt)
+        nc.scalar.activation(warm_up[:], eps_col[:], FUNC.Abs_reciprocal_sqrt)
 
         table_t = held.tile([P, S], BF16, name="table_t")
         for g in range(GROUPS):
@@ -286,36 +285,38 @@ def tile_proteindecoder_b_kernel(
             if step >= LAG and not is_parked(*divmod(step - LAG, F_BLOCKS)):
                 aggregate(*divmod(step - LAG, F_BLOCKS))
 
-        for half in range(2):
-            u_ps.append(psum.tile([P, HALF], F32, name=f"u_ps{half}", tag="bank"))
+        runs = (slice(0, HALF), slice(HALF, HALF + HALF // 2), slice(HALF + HALF // 2, ND))
+        for cols in runs:
+            u_run = psum.tile([P, cols.stop - cols.start], F32, name="u_run", tag="bank")
             for fb in range(F_BLOCKS):
                 nc.tensor.matmul(
-                    u_ps[half][:],
+                    u_run[:],
                     agg[:, fb, :],
-                    wu_sb[fb // 8][:, fb % 8, half * HALF : (half + 1) * HALF],
+                    wu_sb[fb // 8][:, fb % 8, cols],
                     start=(fb == 0),
                     stop=(fb == F_BLOCKS - 1),
                 )
+            u_ps.append(u_run)
 
         y = held.tile([P, ND], F32, name="y")
-        stats = held.tile([P, 2, 6], F32, name="stats")
-        for half in range(2):
-            cols = slice(half * HALF, (half + 1) * HALF)
-            z = work.tile([P, HALF], F32, name="z")
-            nc.vector.tensor_tensor(z[:], u_ps[half][:], bu_all[:, cols], ALU.add)
-            u_sb = work.tile([P, HALF], F32, name="u_sb")
+        stats = held.tile([P, len(runs), 6], F32, name="stats")
+        for k, cols in enumerate(runs):
+            width = cols.stop - cols.start
+            z = work.tile([P, width], F32, name="z")
+            nc.vector.tensor_tensor(z[:], u_ps[k][:], bu_all[:, cols], ALU.add)
+            u_sb = work.tile([P, width], F32, name="u_sb")
             nc.vector.scalar_tensor_tensor(u_sb[:], z[:], SLOPE, z[:], ALU.mult, ALU.max)
             nc.vector.tensor_tensor(y[:, cols], u_sb[:], x_t[:, cols], ALU.add)
-            nc.vector.bn_stats(stats[:, half, :], y[:, cols])
+            nc.vector.bn_stats(stats[:, k, :], y[:, cols])
         mean_var = held.tile([P, 2], F32, name="mean_var")
         nc.vector.bn_aggr(mean_var[:], stats[:].rearrange("q a b -> q (a b)"))
-        std = held.tile([P, 1], F32, name="std")
-        nc.scalar.activation(std[:], mean_var[:, 1:2], FUNC.Sqrt, bias=eps_col[:])
         rstd = held.tile([P, 1], F32, name="rstd")
-        nc.vector.reciprocal(rstd[:], std[:])
+        nc.scalar.activation(rstd[:], mean_var[:, 1:2], FUNC.Abs_reciprocal_sqrt, bias=eps_col[:])
+        neg_mean = held.tile([P, 1], F32, name="neg_mean")
+        nc.vector.tensor_scalar(neg_mean[:], mean_var[:, 0:1], -1.0, None, ALU.mult)
 
         shift = held.tile([P, 1], F32, name="shift")
-        nc.vector.scalar_tensor_tensor(shift[:], mean_var[:, 0:1], -1.0, rstd[:], ALU.mult, ALU.mult)
+        nc.scalar.activation(shift[:], neg_mean[:], FUNC.Identity, scale=rstd[:])
         normal = held.tile([P, ND], F32, name="normal")
         nc.vector.tensor_scalar(
             normal[:, 0:HALF], y[:, 0:HALF], mean_var[:, 0:1], rstd[:], ALU.subtract, ALU.mult

@@ -60,9 +60,10 @@ def tile_proteindecoder_b_kernel(
         wsrc_sb = held.tile([P, D_BLOCKS, M], BF16, name="wsrc_sb")
 
         for g in range(GROUPS):
-            nc.sync.dma_start(table_rows[g][:], table_groups[:, g, :])
+            queue = nc.sync if g % 2 == 0 else nc.scalar
+            queue.dma_start(table_rows[g][:], table_groups[:, g, :])
         nc.sync.dma_start(offsets[:], offs)
-        nc.sync.dma_start(w_sb[:], w)
+        nc.scalar.dma_start(w_sb[:], w)
         vec_rows = held.tile([P, P], F32, name="vec_rows")
         nc.vector.memset(vec_rows[:], 0.0)
         first_row = {}
@@ -75,17 +76,17 @@ def tile_proteindecoder_b_kernel(
             first_row[key] = row
             row += blocks
         nc.sync.dma_start(x_sb[:], x.rearrange("(p c) n -> p c n", p=P))
-        nc.sync.dma_start(wsrc_sb[:], w_src.rearrange("(p c) m -> p c m", p=P))
+        nc.scalar.dma_start(wsrc_sb[:], w_src.rearrange("(p c) m -> p c m", p=P))
         nc.sync.dma_start(wdst_sb[:], w_dst.rearrange("(p c) m -> p c m", p=P))
-        for g in range(2):
-            nc.sync.dma_start(w2_sb[g][:], w2_blocks[:, :, g * (F // 2) : (g + 1) * (F // 2)])
         bu_all = held.tile([P, ND], F32, name="bu_all")
         nc.sync.dma_start(bu_all[:], bu.rearrange("d o -> (d o)").partition_broadcast(P))
         x_blocks = held.tile([P, D_BLOCKS, P], BF16, name="x_blocks")
         nc.sync.dma_start(x_blocks[:], x.rearrange("(c p) n -> p c n", p=P))
 
         for g in range(2):
-            nc.sync.dma_start(
+            nc.gpsimd.dma_start(w2_sb[g][:], w2_blocks[:, :, g * (F // 2) : (g + 1) * (F // 2)])
+        for g in range(2):
+            nc.gpsimd.dma_start(
                 wu_sb[g][:], wu_blocks[:, g * (F_BLOCKS // 2) : (g + 1) * (F_BLOCKS // 2), :]
             )
 

from contextlib import ExitStack

import concourse.mybir as mybir
from concourse.masks import make_identity

BF16 = mybir.dt.bfloat16
F32 = mybir.dt.float32
U16 = mybir.dt.uint16
ALU = mybir.AluOpType
FUNC = mybir.ActivationFunctionType
AXIS = mybir.AxisListType

P = 128
S = 4096
M = 512
F = 2048
ND = 1024
N = 2048
L = 16
PIECE = 512
SLOPE = 0.01
EPS = 1e-5

M_BLOCKS = M // P
F_BLOCKS = F // P
D_BLOCKS = ND // P
PIECES = N // PIECE
NODES = PIECE // L

FLOPS = 2 * (P * M * N + 2 * ND * M * P + M * F * N + F * ND * P)


def tile_proteindecoder_b_kernel(
    tc, table, w, x, w_dst, w_src, b1, w2, b2, wu, bu, gamma, beta, offs, out
):
    nc = tc.nc
    with ExitStack() as ctx:
        held = ctx.enter_context(tc.tile_pool(name="held", bufs=1))
        work = ctx.enter_context(tc.tile_pool(name="work", bufs=4))
        terms = ctx.enter_context(tc.tile_pool(name="terms", bufs=4))
        psum = ctx.enter_context(tc.psum_pool(name="psum", bufs=8))

        ident_bf = held.tile([P, P], BF16, name="ident_bf")
        make_identity(nc, ident_bf[:])
        ident_f32 = held.tile([P, P], F32, name="ident_f32")
        make_identity(nc, ident_f32[:])

        GROUPS = 4
        RUN = S // GROUPS // P
        table_groups = table.rearrange("(g p j) k -> p g (j k)", p=P, j=RUN)
        w2_blocks = w2.rearrange("(c p) f -> p c f", p=P)
        wu_blocks = wu.rearrange("(b p) d -> p b d", p=P)
        table_rows = [held.tile([P, RUN * P], BF16, name=f"table_rows{g}") for g in range(GROUPS)]
        w2_sb = [held.tile([P, M_BLOCKS, F // 2], BF16, name=f"w2_sb{g}") for g in range(2)]
        wu_sb = [held.tile([P, F_BLOCKS // 2, ND], BF16, name=f"wu_sb{g}") for g in range(2)]
        offsets = held.tile([P, N // 16], U16, name="offsets")
        w_sb = held.tile([P, M], BF16, name="w_sb")
        x_sb = held.tile([P, D_BLOCKS, P], BF16, name="x_sb")
        wdst_sb = held.tile([P, D_BLOCKS, M], BF16, name="wdst_sb")
        wsrc_sb = held.tile([P, D_BLOCKS, M], BF16, name="wsrc_sb")

        for g in range(GROUPS):
            queue = nc.sync if g % 2 == 0 else nc.scalar
            queue.dma_start(table_rows[g][:], table_groups[:, g, :])
        nc.sync.dma_start(offsets[:], offs)
        nc.scalar.dma_start(w_sb[:], w)
        vec_rows = held.tile([P, P], F32, name="vec_rows")
        nc.vector.memset(vec_rows[:], 0.0)
        first_row = {}
        row = 0
        for key, vec in (("b1", b1), ("b2", b2), ("gamma", gamma), ("beta", beta)):
            blocks = vec.shape[0] // P
            nc.sync.dma_start(
                vec_rows[row : row + blocks, :], vec.rearrange("(r c) o -> r (c o)", c=P)
            )
            first_row[key] = row
            row += blocks
        nc.sync.dma_start(x_sb[:], x.rearrange("(p c) n -> p c n", p=P))
        nc.scalar.dma_start(wsrc_sb[:], w_src.rearrange("(p c) m -> p c m", p=P))
        nc.sync.dma_start(wdst_sb[:], w_dst.rearrange("(p c) m -> p c m", p=P))
        bu_all = held.tile([P, ND], F32, name="bu_all")
        nc.sync.dma_start(bu_all[:], bu.rearrange("d o -> (d o)").partition_broadcast(P))
        x_blocks = held.tile([P, D_BLOCKS, P], BF16, name="x_blocks")
        nc.sync.dma_start(x_blocks[:], x.rearrange("(c p) n -> p c n", p=P))

        for g in range(2):
            nc.gpsimd.dma_start(w2_sb[g][:], w2_blocks[:, :, g * (F // 2) : (g + 1) * (F // 2)])
        for g in range(2):
            nc.gpsimd.dma_start(
                wu_sb[g][:], wu_blocks[:, g * (F_BLOCKS // 2) : (g + 1) * (F_BLOCKS // 2), :]
            )

        eps_col = held.tile([P, 1], F32, name="eps_col")
        nc.vector.memset(eps_col[:], EPS)
        warm_up = held.tile([P, 1], F32, name="warm_up")
        nc.scalar.activation(warm_up[:], eps_col[:], FUNC.Abs_reciprocal_sqrt)

        table_t = held.tile([P, S], BF16, name="table_t")
        for g in range(GROUPS):
            flipped = psum.tile([P, RUN * P], BF16, name="flipped", tag="bank")
            for j in range(RUN):
                nc.tensor.transpose(
                    flipped[:, j * P : (j + 1) * P],
                    table_rows[g][:, j * P : (j + 1) * P],
                    ident_bf[:],
                )
            target = table_t[:, RUN * P * g : RUN * P * (g + 1)].rearrange("k (p j) -> k p j", j=RUN)
            crosswise = flipped[:].rearrange("k (j p) -> k p j", p=P)
            if g % 2 == 0:
                nc.vector.tensor_copy(target, crosswise)
            else:
                nc.scalar.copy(target, crosswise)

        edge = []

        def look_up(p):
            edge_p = held.tile([P, M_BLOCKS, PIECE], F32, name=f"edge{p}")
            for mb in range(M_BLOCKS):
                e_ps = psum.tile([P, PIECE], F32, name="e_ps", tag="bank")
                nc.tensor.matmul(
                    e_ps[:],
                    w_sb[:, mb * P : (mb + 1) * P],
                    table_t[:].indirect(offsets[:, (PIECE // 16) * p : (PIECE // 16) * (p + 1)]),
                    start=True,
                    stop=True,
                )
                nc.scalar.copy(edge_p[:, mb, :], e_ps[:])
            edge.append(edge_p)

        look_up(0)

        vec_ps = psum.tile([P, P], F32, name="vec_ps", tag="bank")
        nc.tensor.transpose(vec_ps[:], vec_rows[:], ident_f32[:])
        vec_cols = held.tile([P, P], F32, name="vec_cols")
        nc.vector.tensor_copy(vec_cols[:], vec_ps[:])
        slope_cols = held.tile([P, P], F32, name="slope_cols")
        nc.vector.tensor_scalar(slope_cols[:], vec_cols[:], SLOPE, None, ALU.mult)
        steep_cols = held.tile([P, P], F32, name="steep_cols")
        nc.vector.tensor_scalar(steep_cols[:], vec_cols[:], 1.0 - SLOPE, None, ALU.mult)

        def col(key, block):
            c = first_row[key] + block
            return vec_cols[:, c : c + 1]

        def slope_col(key, block):
            c = first_row[key] + block
            return slope_cols[:, c : c + 1]

        def steep_col(key, block):
            c = first_row[key] + block
            return steep_cols[:, c : c + 1]

        q_ps = psum.tile([P, M], F32, name="q_ps", tag="bank")
        r_ps = psum.tile([P, M], F32, name="r_ps", tag="bank")
        for ps, weights in ((q_ps, wsrc_sb), (r_ps, wdst_sb)):
            for mb in range(M_BLOCKS):
                for c in range(D_BLOCKS):
                    nc.tensor.matmul(
                        ps[:, mb * P : (mb + 1) * P],
                        weights[:, c, mb * P : (mb + 1) * P],
                        x_sb[:, c, :],
                        start=(c == 0),
                        stop=(c == D_BLOCKS - 1),
                    )
        qb_sb = held.tile([P, M], F32, name="qb_sb")
        for mb in range(M_BLOCKS):
            nc.scalar.activation(
                qb_sb[:, mb * P : (mb + 1) * P],
                q_ps[:, mb * P : (mb + 1) * P],
                FUNC.Identity,
                bias=col("b1", mb),
            )
        r_sb = held.tile([P, M], F32, name="r_sb")
        nc.vector.tensor_copy(r_sb[:], r_ps[:])

        for p in range(1, PIECES):
            look_up(p)

        PER_BLOCK = F_BLOCKS // M_BLOCKS
        hidden = [held.tile([P, M_BLOCKS, PIECE], BF16, name=f"hidden{p}") for p in range(PIECES)]
        pre_of = {}

        def hidden_sums(p, mb):
            nodes = slice(mb * P + NODES * p, mb * P + NODES * (p + 1))
            shape = [P, NODES // L, L, L]
            by_pair = "q (g i t) -> q g i t"
            adder = nc.vector if p == 0 else nc.gpsimd
            with_sender = terms.tile([P, PIECE], F32, name="with_sender")
            adder.tensor_tensor(
                with_sender[:].rearrange(by_pair, i=L, t=L),
                edge[p][:, mb, :].rearrange(by_pair, i=L, t=L),
                qb_sb[:, nodes].rearrange("q (g t) -> q g t", t=L).unsqueeze(2).to_broadcast(shape),
                ALU.add,
            )
            pre = work.tile([P, PIECE], F32, name="pre")
            adder.tensor_tensor(
                pre[:].rearrange(by_pair, i=L, t=L),
                with_sender[:].rearrange(by_pair, i=L, t=L),
                r_sb[:, nodes].rearrange("q (g i) -> q g i", i=L).unsqueeze(3).to_broadcast(shape),
                ALU.add,
            )
            pre_of[(p, mb)] = pre

        def hidden_relu(p, mb):
            pre = pre_of[(p, mb)]
            nc.vector.scalar_tensor_tensor(
                hidden[p][:, mb, :], pre[:], SLOPE, pre[:], ALU.mult, ALU.max
            )

        agg = held.tile([P, F_BLOCKS, P], BF16, name="agg")
        HALF = ND // 2
        u_ps = []
        summands = {}

        LATE = PIECES // 2

        def without_vector(p, fb):
            return p >= LATE and fb % 2 == 1

        def is_parked(p, fb):
            return p < LATE and fb % PER_BLOCK == PER_BLOCK - 1

        def messages(p, fb):
            m_ps = psum.tile([P, PIECE], F32, name="m_ps", tag="bank")
            for c in range(M_BLOCKS):
                nc.tensor.matmul(
                    m_ps[:],
                    w2_sb[fb // 8][:, c, (fb % 8) * P : (fb % 8 + 1) * P],
                    hidden[p][:, c, :],
                    start=(c == 0),
                    stop=(c == M_BLOCKS - 1),
                )
            low = work.tile([P, PIECE], F32, name="low")
            nc.scalar.activation(
                low[:], m_ps[:], FUNC.Identity, bias=slope_col("b2", fb), scale=SLOPE
            )
            if is_parked(p, fb):
                msg = held.tile([P, PIECE], F32, name=f"parked{p}_{fb}")
            else:
                msg = work.tile([P, PIECE], F32, name="msg")
            if without_vector(p, fb):
                steep = work.tile([P, PIECE], F32, name="steep")
                nc.scalar.activation(
                    steep[:], m_ps[:], FUNC.Relu, bias=steep_col("b2", fb), scale=1.0 - SLOPE
                )
                nc.gpsimd.tensor_tensor(msg[:], steep[:], low[:], ALU.add)
            else:
                nc.vector.scalar_tensor_tensor(
                    msg[:], m_ps[:], col("b2", fb), low[:], ALU.add, ALU.max
                )
            senders = msg[:].rearrange("q (n t) -> q n t", t=L)
            summands[(p, fb)] = senders

        def aggregate(p, fb):
            with nc.allow_low_precision(reason="summed in float32, rounded once to bfloat16"):
                nc.vector.tensor_reduce(
                    agg[:, fb, NODES * p : NODES * (p + 1)], summands[(p, fb)], AXIS.X, ALU.add
                )

        x_t = held.tile([P, ND], BF16, name="x_t")

        def turn_x():
            xt_ps = psum.tile([P, ND], BF16, name="xt_ps", tag="bank")
            for c in range(D_BLOCKS):
                nc.tensor.transpose(xt_ps[:, c * P : (c + 1) * P], x_blocks[:, c, :], ident_bf[:])
            nc.scalar.copy(x_t[:], xt_ps[:])

        for mb in range(M_BLOCKS):
            hidden_sums(0, mb)
            hidden_relu(0, mb)

        STEPS = PIECES * F_BLOCKS
        LAG = 2
        for step in range(STEPS + LAG):
            if step < STEPS:
                p, fb = divmod(step, F_BLOCKS)
                if p == 1 and fb == 0:
                    turn_x()
                messages(p, fb)
                if p + 1 < PIECES and fb % PER_BLOCK == 0:
                    hidden_sums(p + 1, fb // PER_BLOCK)
                if p + 1 < PIECES and fb % PER_BLOCK == PER_BLOCK - 1:
                    hidden_relu(p + 1, fb // PER_BLOCK)
                if p >= LATE and is_parked(p - LATE, fb):
                    aggregate(p - LATE, fb)
            if step >= LAG and not is_parked(*divmod(step - LAG, F_BLOCKS)):
                aggregate(*divmod(step - LAG, F_BLOCKS))

        runs = (slice(0, HALF), slice(HALF, HALF + HALF // 2), slice(HALF + HALF // 2, ND))
        for cols in runs:
            u_run = psum.tile([P, cols.stop - cols.start], F32, name="u_run", tag="bank")
            for fb in range(F_BLOCKS):
                nc.tensor.matmul(
                    u_run[:],
                    agg[:, fb, :],
                    wu_sb[fb // 8][:, fb % 8, cols],
                    start=(fb == 0),
                    stop=(fb == F_BLOCKS - 1),
                )
            u_ps.append(u_run)

        y = held.tile([P, ND], F32, name="y")
        stats = held.tile([P, len(runs), 6], F32, name="stats")
        for k, cols in enumerate(runs):
            width = cols.stop - cols.start
            z = work.tile([P, width], F32, name="z")
            nc.vector.tensor_tensor(z[:], u_ps[k][:], bu_all[:, cols], ALU.add)
            u_sb = work.tile([P, width], F32, name="u_sb")
            nc.vector.scalar_tensor_tensor(u_sb[:], z[:], SLOPE, z[:], ALU.mult, ALU.max)
            nc.vector.tensor_tensor(y[:, cols], u_sb[:], x_t[:, cols], ALU.add)
            nc.vector.bn_stats(stats[:, k, :], y[:, cols])
        mean_var = held.tile([P, 2], F32, name="mean_var")
        nc.vector.bn_aggr(mean_var[:], stats[:].rearrange("q a b -> q (a b)"))
        rstd = held.tile([P, 1], F32, name="rstd")
        nc.scalar.activation(rstd[:], mean_var[:, 1:2], FUNC.Abs_reciprocal_sqrt, bias=eps_col[:])
        neg_mean = held.tile([P, 1], F32, name="neg_mean")
        nc.vector.tensor_scalar(neg_mean[:], mean_var[:, 0:1], -1.0, None, ALU.mult)

        shift = held.tile([P, 1], F32, name="shift")
        nc.scalar.activation(shift[:], neg_mean[:], FUNC.Identity, scale=rstd[:])
        normal = held.tile([P, ND], F32, name="normal")
        nc.vector.tensor_scalar(
            normal[:, 0:HALF], y[:, 0:HALF], mean_var[:, 0:1], rstd[:], ALU.subtract, ALU.mult
        )
        nc.scalar.activation(
            normal[:, HALF:ND], y[:, HALF:ND], FUNC.Identity, bias=shift[:], scale=rstd[:]
        )

        result = held.tile([P, D_BLOCKS, P], F32, name="result")
        out_blocks = out.rearrange("(c p) n -> p c n", p=P)
        for db in range(D_BLOCKS):
            turned = psum.tile([P, P], F32, name="turned", tag="bank")
            nc.tensor.transpose(turned[:], normal[:, db * P : (db + 1) * P], ident_f32[:])
            if db % 2 == 0:
                nc.scalar.activation(
                    result[:, db, :], turned[:], FUNC.Identity, bias=col("beta", db), scale=col("gamma", db)
                )
            else:
                nc.vector.tensor_scalar(
                    result[:, db, :], turned[:], col("gamma", db), col("beta", db), ALU.mult, ALU.add
                )
            if db % 2 == 1:
                nc.sync.dma_start(out_blocks[:, db - 1 : db + 1, :], result[:, db - 1 : db + 1, :])
